import numpy as np
import ml_dtypes


def mxq(x, axis, fmt="e4m3"):
    dtype, down = {"e4m3": (ml_dtypes.float8_e4m3fn, 7), "e5m2": (ml_dtypes.float8_e5m2, 14)}[fmt]
    v = np.moveaxis(np.asarray(x, np.float32).astype(ml_dtypes.bfloat16).astype(np.float64), axis, -1)
    blocks = v.reshape(v.shape[:-1] + (-1, 32))
    amax = np.abs(blocks).max(-1, keepdims=True)
    byte = np.maximum(np.where(amax > 0, np.frexp(amax)[1] - 1 + 127, 0) - down, 1)
    scale = np.exp2(byte - 127.0)
    codes = (blocks / scale).astype(np.float32).astype(dtype).astype(np.float64)
    return np.moveaxis((codes * scale).reshape(v.shape), -1, axis)


WIDE = False


def mx_kscale(k):
    if not WIDE:
        return np.ones(k)
    levels = np.array([10, -10, 5, -5, 0])
    a = np.random.permutation(np.resize(levels, k // 512 * 4)).reshape(k // 512, 4)
    idx = np.arange(k)
    return np.exp2(a[idx // 512, idx % 128 // 32])


BF16 = ml_dtypes.bfloat16


def bf(x):
    return np.asarray(x, np.float32).astype(BF16)


def f64(x):
    return np.asarray(x).astype(np.float64)


B, C, T, P, N, D = 8, 16, 1024, 128, 8, 8192
L = T // P
G = L // N


def setup_inputs():
    s = mx_kscale(D)
    u = mx_kscale(P * N)
    un = u.reshape(P, N).T
    ut = np.tile(u, G)
    return {'h_enc': bf(np.random.standard_normal((N, B, C, G, D)) * 0.7 * s),
            'dec_W': bf(np.random.standard_normal((N, D, P)) / np.sqrt(D) / s[None, :, None] * un[:, None, :]),
            'dec_b': bf(np.random.standard_normal((N, P)) * 0.2 * un),
            'map_W': bf(np.random.standard_normal((T, T)) / np.sqrt(T) / ut[:, None]),
            'map_b': bf(np.random.standard_normal(T) * 0.2)}


def reference(h_enc, dec_W, dec_b, map_W, map_b):
    h = f64(h_enc).reshape(N, B * C * G, D)
    r = (mxq(h, 2, 'e4m3') @ mxq(f64(dec_W), 1, 'e4m3')) + f64(dec_b)[:, None, :]
    r = r.reshape(N, B, C, G * P)
    x_rec = np.moveaxis(r, 0, -1).reshape(B * C, T)
    y_hat = (mxq(x_rec, 1, 'e4m3') @ mxq(f64(map_W), 0, 'e4m3')) + f64(map_b)
    return y_hat.reshape(B, C, T)

@@ -1,0 +1,249 @@
+from contextlib import ExitStack
+
+import concourse.mybir as mybir
+from concourse.masks import make_identity
+
+BF16 = mybir.dt.bfloat16
+F32 = mybir.dt.float32
+I32 = mybir.dt.int32
+U32 = mybir.dt.uint32
+U8 = mybir.dt.uint8
+FP8X4 = mybir.dt.float8_e4m3fn_x4
+ADD = mybir.AluOpType.add
+
+P = 128
+PACK = 4
+K_PASS = P * PACK
+
+MODELS = 8
+ROWS = 128
+FEATURES = 8192
+SAMPLES = 128
+TIME = MODELS * SAMPLES
+
+CHUNK_PASSES = 4
+CHUNK_K = CHUNK_PASSES * K_PASS
+CHUNKS_PER_MODEL = FEATURES // CHUNK_K
+CHUNKS = MODELS * CHUNKS_PER_MODEL
+BANK_PASSES = 2
+LOADS_AHEAD = 8
+
+W_COLS_SCALAR = 32
+W_COLS_VECTOR = SAMPLES - W_COLS_SCALAR
+
+TIME_PASSES = TIME // K_PASS
+N_HALF = 512
+HALVES = TIME // N_HALF
+
+FLOPS = 2 * MODELS * ROWS * FEATURES * SAMPLES + 2 * ROWS * TIME * TIME
+
+
+def tile_model_pb_k_kernel(tc, h_enc, dec_W, dec_b, map_W, map_b, out):
+    nc = tc.nc
+    h_rows = h_enc.rearrange("n b c l d -> n (b c l) d")
+    out_rows = out.rearrange("b c s -> (b c) s")
+
+    with ExitStack() as ctx:
+        keep = ctx.enter_context(tc.tile_pool(name="keep", bufs=1))
+        h_pool = ctx.enter_context(tc.tile_pool(name="h_pool", bufs=3))
+        w_pool = ctx.enter_context(tc.tile_pool(name="w_pool", bufs=LOADS_AHEAD))
+        stage = ctx.enter_context(tc.tile_pool(name="stage", bufs=4))
+        psum_t = ctx.enter_context(tc.psum_pool(name="psum_t", bufs=4))
+        psum_r = ctx.enter_context(tc.psum_pool(name="psum_r", bufs=2))
+        psum_w = ctx.enter_context(tc.psum_pool(name="psum_w", bufs=2))
+        ctx.enter_context(tc.manual_schedule())
+
+        h_raw = {}
+        w_raw = {}
+        h_grouped = {}
+        w_grouped = {}
+        h_mx = {}
+        w_mx = {}
+        r_acc = {}
+
+        def load_chunk(i):
+            n, c = divmod(i, CHUNKS_PER_MODEL)
+            if c == 0:
+                rows = h_pool.tile([ROWS, FEATURES], BF16, name="h_rows_sb")
+                nc.sync.dma_start(out=rows[:], in_=h_rows[n])
+                h_raw[n] = rows
+            w_rows = w_pool.tile([P, CHUNK_PASSES, PACK, SAMPLES], BF16, name="w_rows_sb")
+            nc.sync.dma_start(
+                out=w_rows[:].rearrange("q c j w -> q c (j w)"),
+                in_=dec_W[n, c * CHUNK_K : (c + 1) * CHUNK_K, :].rearrange(
+                    "(c q j) w -> q c (j w)", q=P, j=PACK
+                ),
+            )
+            w_raw[i] = w_rows
+
+        def transpose_h(i):
+            n, c = divmod(i, CHUNKS_PER_MODEL)
+            words = h_raw[n][:].bitcast(F32).rearrange("r (c q u) -> r c u q", q=P, u=2)
+            grouped = stage.tile([P, CHUNK_PASSES * ROWS * PACK], BF16, name="h_grouped_sb", align_bytes=64)
+            grouped_words = grouped[:].bitcast(F32).rearrange("q (c r u) -> q c r u", c=CHUNK_PASSES, u=2)
+            for b in range(CHUNK_PASSES // BANK_PASSES):
+                bank = psum_t.tile([P, BANK_PASSES, 2, ROWS], F32, name="h_bank")
+                for cb in range(BANK_PASSES):
+                    for u in range(2):
+                        nc.tensor.transpose(
+                            bank[:, cb, u, :],
+                            words[:, c * CHUNK_PASSES + b * BANK_PASSES + cb, u, :],
+                            ident_f32[:],
+                        )
+                nc.scalar.copy(
+                    out=grouped_words[:, b * BANK_PASSES : (b + 1) * BANK_PASSES],
+                    in_=bank[:].rearrange("q c u r -> q c r u"),
+                )
+            h_grouped[i] = grouped[:]
+
+        def regroup_w(i):
+            grouped = stage.tile([P, CHUNK_PASSES, SAMPLES, PACK], BF16, name="w_grouped_sb", align_bytes=64)
+            nc.vector.tensor_copy(
+                out=grouped[:, :, 0:W_COLS_VECTOR, :].rearrange("q c (g i) j -> q c g j i", i=4),
+                in_=w_raw[i][:, :, :, 0:W_COLS_VECTOR].rearrange("q c j (g i) -> q c g j i", i=4),
+            )
+            nc.scalar.copy(
+                out=grouped[:, :, W_COLS_VECTOR:SAMPLES, :],
+                in_=w_raw[i][:, :, :, W_COLS_VECTOR:SAMPLES].rearrange("q c j w -> q c w j"),
+            )
+            w_grouped[i] = grouped[:].rearrange("q c w j -> q (c w j)")
+
+        def quantise(values, operand):
+            words = stage.tile([P, CHUNK_PASSES * P], U32, tag=operand + "_words", align_bytes=64)
+            scales = stage.tile([P, CHUNK_PASSES * P], U8, tag=operand + "_scales", align_bytes=64)
+            nc.vector.quantize_mx(out=words[:].bitcast(FP8X4), scales=scales[:], in_=values)
+            return words, scales
+
+        def multiply(i):
+            n, c = divmod(i, CHUNKS_PER_MODEL)
+            if c == 0:
+                acc = psum_r.tile([ROWS, SAMPLES], F32, name="r_sums")
+                r_acc[n] = acc
+            h_words, h_scales = h_mx[i]
+            w_words, w_scales = w_mx[i]
+            for cp in range(CHUNK_PASSES):
+                cols = slice(cp * P, (cp + 1) * P)
+                nc.tensor.matmul_mx(
+                    out=r_acc[n][:],
+                    lhsT=h_words[:, cols].bitcast(FP8X4),
+                    lhsT_scale=h_scales[:, cols],
+                    rhs=w_words[:, cols].bitcast(FP8X4),
+                    rhs_scale=w_scales[:, cols],
+                    start=(c == 0 and cp == 0),
+                    stop=(c == CHUNKS_PER_MODEL - 1 and cp == CHUNK_PASSES - 1),
+                )
+            if c == CHUNKS_PER_MODEL - 1:
+                finish_model(n)
+
+        def finish_model(n):
+            nc.vector.tensor_tensor(
+                out=x_sb[:].rearrange("r (g j m a) -> r g j m a", g=TIME_PASSES, j=PACK, a=2)[:, :, n % PACK, :, n // PACK],
+                in0=r_acc[n][:].rearrange("r (g m) -> r g m", g=TIME_PASSES),
+                in1=bias_sb[:, n * SAMPLES : (n + 1) * SAMPLES].rearrange("r (g m) -> r g m", g=TIME_PASSES),
+                op=ADD,
+            )
+
+        def transpose_x(j):
+            for g in range(TIME_PASSES):
+                first = (g * PACK + j) * P
+                nc.tensor.transpose(x_bank[g][:, j, :], x_sb[:, first : first + P], ident_bf16[:])
+
+        ident_f32 = keep.tile([P, P], F32)
+        make_identity(nc, ident_f32[:])
+        ident_bf16 = keep.tile([P, P], BF16)
+        make_identity(nc, ident_bf16[:])
+
+        m_raw = keep.tile([P, TIME_PASSES, PACK, TIME], BF16)
+        for g in range(TIME_PASSES):
+            nc.sync.dma_start(
+                out=m_raw[:, g],
+                in_=map_W[g * K_PASS : (g + 1) * K_PASS, :].rearrange("(q j) s -> q j s", j=PACK),
+            )
+        for i in range(LOADS_AHEAD):
+            load_chunk(i)
+
+        bias_rows = keep.tile([P, 2 * TIME], BF16)
+        nc.vector.memset(bias_rows[:].bitcast(I32), 0)
+        ones = keep.tile([P, P], BF16)
+        nc.vector.memset(ones[:], 1.0)
+        nc.scalar.dma_start(out=bias_rows[0:1, 0:TIME], in_=dec_b.rearrange("n p -> (n p)").unsqueeze(0))
+        nc.scalar.dma_start(out=bias_rows[0:1, TIME : 2 * TIME], in_=map_b.unsqueeze(0))
+        bias_sb = keep.tile([P, 2 * TIME], F32)
+        for b in range(2 * TIME // N_HALF):
+            cols = slice(b * N_HALF, (b + 1) * N_HALF)
+            bias_bank = psum_w.tile([P, N_HALF], F32, tag="wide")
+            nc.tensor.matmul(out=bias_bank[:], lhsT=ones[:], rhs=bias_rows[:, cols], start=True, stop=True)
+            nc.scalar.copy(out=bias_sb[:, cols], in_=bias_bank[:])
+
+        m_grouped = keep.tile([P, TIME_PASSES, TIME, PACK], BF16, align_bytes=64)
+        m_words = keep.tile([P, TIME_PASSES, TIME], U32, align_bytes=64)
+        m_scales = keep.tile([P, TIME_PASSES, TIME], U8, align_bytes=64)
+        for g in range(TIME_PASSES):
+            nc.vector.tensor_copy(
+                out=m_grouped[:, g].rearrange("q (c i) j -> q c j i", i=4),
+                in_=m_raw[:, g].rearrange("q j (c i) -> q c j i", i=4),
+            )
+        for g in range(TIME_PASSES):
+            nc.vector.quantize_mx(
+                out=m_words[:, g].bitcast(FP8X4),
+                scales=m_scales[:, g],
+                in_=m_grouped[:, g].rearrange("q s j -> q (s j)"),
+            )
+
+        x_sb = keep.tile([ROWS, TIME], BF16)
+        for i in range(-2, CHUNKS):
+            if 0 <= i + 2 < CHUNKS:
+                transpose_h(i + 2)
+            if 0 <= i < CHUNKS:
+                regroup_w(i)
+            if 0 <= i + 1 < CHUNKS:
+                h_mx[i + 1] = quantise(h_grouped[i + 1], "h")
+            if 0 <= i < CHUNKS:
+                w_mx[i] = quantise(w_grouped[i], "w")
+            if 0 <= i - 1 < CHUNKS:
+                multiply(i - 1)
+            if 0 <= i and i + LOADS_AHEAD < CHUNKS:
+                load_chunk(i + LOADS_AHEAD)
+        x_bank = []
+        for g in range(TIME_PASSES):
+            bank = psum_w.tile([P, PACK, ROWS], BF16, tag="wide")
+            x_bank.append(bank)
+        for j in range(PACK - 1):
+            transpose_x(j)
+        multiply(CHUNKS - 1)
+        transpose_x(PACK - 1)
+
+        x_grouped = keep.tile([P, TIME_PASSES, ROWS, PACK], BF16, align_bytes=64)
+        x_words = keep.tile([P, TIME_PASSES, ROWS], U32, align_bytes=64)
+        x_scales = keep.tile([P, TIME_PASSES, ROWS], U8, align_bytes=64)
+        nc.vector.tensor_copy(out=x_grouped[:, 0], in_=x_bank[0][:].rearrange("q j r -> q r j"))
+        nc.scalar.copy(out=x_grouped[:, 1], in_=x_bank[1][:].rearrange("q j r -> q r j"))
+        for g in range(TIME_PASSES):
+            nc.vector.quantize_mx(
+                out=x_words[:, g].bitcast(FP8X4),
+                scales=x_scales[:, g],
+                in_=x_grouped[:, g].rearrange("q r j -> q (r j)"),
+            )
+        y_acc = []
+        for half in range(HALVES):
+            y_bank = psum_w.tile([ROWS, N_HALF], F32, tag="wide")
+            y_acc.append(y_bank)
+        for g in range(TIME_PASSES):
+            for half in range(HALVES):
+                cols = slice(half * N_HALF, (half + 1) * N_HALF)
+                nc.tensor.matmul_mx(
+                    out=y_acc[half][:],
+                    lhsT=x_words[:, g].bitcast(FP8X4),
+                    lhsT_scale=x_scales[:, g],
+                    rhs=m_words[:, g, cols].bitcast(FP8X4),
+                    rhs_scale=m_scales[:, g, cols],
+                    start=(g == 0),
+                    stop=(g == TIME_PASSES - 1),
+                )
+        for half in range(HALVES):
+            cols = slice(half * N_HALF, (half + 1) * N_HALF)
+            y_sb = stage.tile([ROWS, N_HALF], F32)
+            nc.vector.tensor_tensor(
+                out=y_sb[:], in0=y_acc[half][:], in1=bias_sb[:, TIME + half * N_HALF : TIME + (half + 1) * N_HALF], op=ADD
+            )
+            nc.sync.dma_start(out=out_rows[:, cols], in_=y_sb[:])

@@ -28,7 +28,7 @@ CHUNKS = MODELS * CHUNKS_PER_MODEL
 BANK_PASSES = 2
 LOADS_AHEAD = 8
 
-W_COLS_SCALAR = 32
+W_COLS_SCALAR = 48
 W_COLS_VECTOR = SAMPLES - W_COLS_SCALAR
 
 TIME_PASSES = TIME // K_PASS

@@ -28,7 +28,7 @@ CHUNKS = MODELS * CHUNKS_PER_MODEL
 BANK_PASSES = 2
 LOADS_AHEAD = 8
 
-W_COLS_SCALAR = 48
+W_COLS_SCALAR = 32
 W_COLS_VECTOR = SAMPLES - W_COLS_SCALAR
 
 TIME_PASSES = TIME // K_PASS
@@ -45,8 +45,7 @@ def tile_model_pb_k_kernel(tc, h_enc, dec_W, dec_b, map_W, map_b, out):
 
     with ExitStack() as ctx:
         keep = ctx.enter_context(tc.tile_pool(name="keep", bufs=1))
-        h_pool = ctx.enter_context(tc.tile_pool(name="h_pool", bufs=3))
-        w_pool = ctx.enter_context(tc.tile_pool(name="w_pool", bufs=LOADS_AHEAD))
+        loads = ctx.enter_context(tc.tile_pool(name="loads", bufs=LOADS_AHEAD))
         stage = ctx.enter_context(tc.tile_pool(name="stage", bufs=4))
         psum_t = ctx.enter_context(tc.psum_pool(name="psum_t", bufs=4))
         psum_r = ctx.enter_context(tc.psum_pool(name="psum_r", bufs=2))
@@ -63,22 +62,19 @@ def tile_model_pb_k_kernel(tc, h_enc, dec_W, dec_b, map_W, map_b, out):
 
         def load_chunk(i):
             n, c = divmod(i, CHUNKS_PER_MODEL)
-            if c == 0:
-                rows = h_pool.tile([ROWS, FEATURES], BF16, name="h_rows_sb")
-                nc.sync.dma_start(out=rows[:], in_=h_rows[n])
-                h_raw[n] = rows
-            w_rows = w_pool.tile([P, CHUNK_PASSES, PACK, SAMPLES], BF16, name="w_rows_sb")
+            features = slice(c * CHUNK_K, (c + 1) * CHUNK_K)
+            h_part = loads.tile([ROWS, CHUNK_K], BF16)
+            nc.sync.dma_start(out=h_part[:], in_=h_rows[n, :, features])
+            h_raw[i] = h_part
+            w_part = loads.tile([P, CHUNK_PASSES, PACK, SAMPLES], BF16)
             nc.sync.dma_start(
-                out=w_rows[:].rearrange("q c j w -> q c (j w)"),
-                in_=dec_W[n, c * CHUNK_K : (c + 1) * CHUNK_K, :].rearrange(
-                    "(c q j) w -> q c (j w)", q=P, j=PACK
-                ),
+                out=w_part[:].rearrange("q c j w -> q c (j w)"),
+                in_=dec_W[n, features, :].rearrange("(c q j) w -> q c (j w)", q=P, j=PACK),
             )
-            w_raw[i] = w_rows
+            w_raw[i] = w_part
 
         def transpose_h(i):
-            n, c = divmod(i, CHUNKS_PER_MODEL)
-            words = h_raw[n][:].bitcast(F32).rearrange("r (c q u) -> r c u q", q=P, u=2)
+            words = h_raw[i][:].bitcast(F32).rearrange("r (c q u) -> r c u q", q=P, u=2)
             grouped = stage.tile([P, CHUNK_PASSES * ROWS * PACK], BF16, name="h_grouped_sb", align_bytes=64)
             grouped_words = grouped[:].bitcast(F32).rearrange("q (c r u) -> q c r u", c=CHUNK_PASSES, u=2)
             for b in range(CHUNK_PASSES // BANK_PASSES):
@@ -87,7 +83,7 @@ def tile_model_pb_k_kernel(tc, h_enc, dec_W, dec_b, map_W, map_b, out):
                     for u in range(2):
                         nc.tensor.transpose(
                             bank[:, cb, u, :],
-                            words[:, c * CHUNK_PASSES + b * BANK_PASSES + cb, u, :],
+                            words[:, b * BANK_PASSES + cb, u, :],
                             ident_f32[:],
                         )
                 nc.scalar.copy(
@@ -132,8 +128,6 @@ def tile_model_pb_k_kernel(tc, h_enc, dec_W, dec_b, map_W, map_b, out):
                     start=(c == 0 and cp == 0),
                     stop=(c == CHUNKS_PER_MODEL - 1 and cp == CHUNK_PASSES - 1),
                 )
-            if c == CHUNKS_PER_MODEL - 1:
-                finish_model(n)
 
         def finish_model(n):
             nc.vector.tensor_tensor(
@@ -191,18 +185,16 @@ def tile_model_pb_k_kernel(tc, h_enc, dec_W, dec_b, map_W, map_b, out):
             )
 
         x_sb = keep.tile([ROWS, TIME], BF16)
-        for i in range(-2, CHUNKS):
-            if 0 <= i + 2 < CHUNKS:
-                transpose_h(i + 2)
-            if 0 <= i < CHUNKS:
-                regroup_w(i)
-            if 0 <= i + 1 < CHUNKS:
-                h_mx[i + 1] = quantise(h_grouped[i + 1], "h")
-            if 0 <= i < CHUNKS:
-                w_mx[i] = quantise(w_grouped[i], "w")
-            if 0 <= i - 1 < CHUNKS:
+        for i in range(CHUNKS):
+            transpose_h(i)
+            if i > 0:
                 multiply(i - 1)
-            if 0 <= i and i + LOADS_AHEAD < CHUNKS:
+            regroup_w(i)
+            h_mx[i] = quantise(h_grouped[i], "h")
+            w_mx[i] = quantise(w_grouped[i], "w")
+            if i > 0 and i % CHUNKS_PER_MODEL == 0:
+                finish_model(i // CHUNKS_PER_MODEL - 1)
+            if i + LOADS_AHEAD < CHUNKS:
                 load_chunk(i + LOADS_AHEAD)
         x_bank = []
         for g in range(TIME_PASSES):
@@ -211,6 +203,7 @@ def tile_model_pb_k_kernel(tc, h_enc, dec_W, dec_b, map_W, map_b, out):
         for j in range(PACK - 1):
             transpose_x(j)
         multiply(CHUNKS - 1)
+        finish_model(MODELS - 1)
         transpose_x(PACK - 1)
 
         x_grouped = keep.tile([P, TIME_PASSES, ROWS, PACK], BF16, align_bytes=64)
@@ -228,8 +221,8 @@ def tile_model_pb_k_kernel(tc, h_enc, dec_W, dec_b, map_W, map_b, out):
         for half in range(HALVES):
             y_bank = psum_w.tile([ROWS, N_HALF], F32, tag="wide")
             y_acc.append(y_bank)
-        for g in range(TIME_PASSES):
-            for half in range(HALVES):
+        for half in range(HALVES):
+            for g in range(TIME_PASSES):
                 cols = slice(half * N_HALF, (half + 1) * N_HALF)
                 nc.tensor.matmul_mx(
                     out=y_acc[half][:],

@@ -28,8 +28,8 @@ CHUNKS = MODELS * CHUNKS_PER_MODEL
 BANK_PASSES = 2
 LOADS_AHEAD = 8
 
-W_COLS_SCALAR = 32
-W_COLS_VECTOR = SAMPLES - W_COLS_SCALAR
+W_COLS_VECTOR = SAMPLES * 5 // 8
+M_COLS_VECTOR = TIME * 5 // 8
 
 TIME_PASSES = TIME // K_PASS
 N_HALF = 512
@@ -137,6 +137,31 @@ def tile_model_pb_k_kernel(tc, h_enc, dec_W, dec_b, map_W, map_b, out):
                 op=ADD,
             )
 
+        def load_map(g):
+            nc.sync.dma_start(
+                out=m_raw[:, g],
+                in_=map_W[g * K_PASS : (g + 1) * K_PASS, :].rearrange("(q j) s -> q j s", j=PACK),
+            )
+
+        def regroup_map(g):
+            nc.vector.tensor_copy(
+                out=m_grouped[:, g, 0:M_COLS_VECTOR, :].rearrange("q (c i) j -> q c j i", i=4),
+                in_=m_raw[:, g, :, 0:M_COLS_VECTOR].rearrange("q j (c i) -> q c j i", i=4),
+            )
+            nc.scalar.copy(
+                out=m_grouped[:, g, M_COLS_VECTOR:TIME, :],
+                in_=m_raw[:, g, :, M_COLS_VECTOR:TIME].rearrange("q j s -> q s j"),
+            )
+
+        def quantise_map(g):
+            for half in range(HALVES):
+                cols = slice(half * N_HALF, (half + 1) * N_HALF)
+                nc.vector.quantize_mx(
+                    out=m_words[:, g, cols].bitcast(FP8X4),
+                    scales=m_scales[:, g, cols],
+                    in_=m_grouped[:, g, cols, :].rearrange("q s j -> q (s j)"),
+                )
+
         def transpose_x(j):
             for g in range(TIME_PASSES):
                 first = (g * PACK + j) * P
@@ -147,21 +172,21 @@ def tile_model_pb_k_kernel(tc, h_enc, dec_W, dec_b, map_W, map_b, out):
         ident_bf16 = keep.tile([P, P], BF16)
         make_identity(nc, ident_bf16[:])
 
-        m_raw = keep.tile([P, TIME_PASSES, PACK, TIME], BF16)
-        for g in range(TIME_PASSES):
-            nc.sync.dma_start(
-                out=m_raw[:, g],
-                in_=map_W[g * K_PASS : (g + 1) * K_PASS, :].rearrange("(q j) s -> q j s", j=PACK),
-            )
-        for i in range(LOADS_AHEAD):
-            load_chunk(i)
-
         bias_rows = keep.tile([P, 2 * TIME], BF16)
         nc.vector.memset(bias_rows[:].bitcast(I32), 0)
         ones = keep.tile([P, P], BF16)
         nc.vector.memset(ones[:], 1.0)
-        nc.scalar.dma_start(out=bias_rows[0:1, 0:TIME], in_=dec_b.rearrange("n p -> (n p)").unsqueeze(0))
-        nc.scalar.dma_start(out=bias_rows[0:1, TIME : 2 * TIME], in_=map_b.unsqueeze(0))
+        nc.sync.dma_start(out=bias_rows[0:1, 0:TIME], in_=dec_b.rearrange("n p -> (n p)").unsqueeze(0))
+        nc.sync.dma_start(out=bias_rows[0:1, TIME : 2 * TIME], in_=map_b.unsqueeze(0))
+
+        m_raw = keep.tile([P, TIME_PASSES, PACK, TIME], BF16)
+        m_grouped = keep.tile([P, TIME_PASSES, TIME, PACK], BF16, align_bytes=64)
+        m_words = keep.tile([P, TIME_PASSES, TIME], U32, align_bytes=64)
+        m_scales = keep.tile([P, TIME_PASSES, TIME], U8, align_bytes=64)
+        load_map(0)
+        for i in range(LOADS_AHEAD):
+            load_chunk(i)
+
         bias_sb = keep.tile([P, 2 * TIME], F32)
         for b in range(2 * TIME // N_HALF):
             cols = slice(b * N_HALF, (b + 1) * N_HALF)
@@ -169,20 +194,8 @@ def tile_model_pb_k_kernel(tc, h_enc, dec_W, dec_b, map_W, map_b, out):
             nc.tensor.matmul(out=bias_bank[:], lhsT=ones[:], rhs=bias_rows[:, cols], start=True, stop=True)
             nc.scalar.copy(out=bias_sb[:, cols], in_=bias_bank[:])
 
-        m_grouped = keep.tile([P, TIME_PASSES, TIME, PACK], BF16, align_bytes=64)
-        m_words = keep.tile([P, TIME_PASSES, TIME], U32, align_bytes=64)
-        m_scales = keep.tile([P, TIME_PASSES, TIME], U8, align_bytes=64)
-        for g in range(TIME_PASSES):
-            nc.vector.tensor_copy(
-                out=m_grouped[:, g].rearrange("q (c i) j -> q c j i", i=4),
-                in_=m_raw[:, g].rearrange("q j (c i) -> q c j i", i=4),
-            )
-        for g in range(TIME_PASSES):
-            nc.vector.quantize_mx(
-                out=m_words[:, g].bitcast(FP8X4),
-                scales=m_scales[:, g],
-                in_=m_grouped[:, g].rearrange("q s j -> q (s j)"),
-            )
+        regroup_map(0)
+        quantise_map(0)
 
         x_sb = keep.tile([ROWS, TIME], BF16)
         for i in range(CHUNKS):
@@ -196,6 +209,7 @@ def tile_model_pb_k_kernel(tc, h_enc, dec_W, dec_b, map_W, map_b, out):
                 finish_model(i // CHUNKS_PER_MODEL - 1)
             if i + LOADS_AHEAD < CHUNKS:
                 load_chunk(i + LOADS_AHEAD)
+        load_map(1)
         x_bank = []
         for g in range(TIME_PASSES):
             bank = psum_w.tile([P, PACK, ROWS], BF16, tag="wide")
@@ -203,6 +217,7 @@ def tile_model_pb_k_kernel(tc, h_enc, dec_W, dec_b, map_W, map_b, out):
         for j in range(PACK - 1):
             transpose_x(j)
         multiply(CHUNKS - 1)
+        regroup_map(1)
         finish_model(MODELS - 1)
         transpose_x(PACK - 1)
 
@@ -217,12 +232,13 @@ def tile_model_pb_k_kernel(tc, h_enc, dec_W, dec_b, map_W, map_b, out):
                 scales=x_scales[:, g],
                 in_=x_grouped[:, g].rearrange("q r j -> q (r j)"),
             )
+        quantise_map(1)
         y_acc = []
         for half in range(HALVES):
             y_bank = psum_w.tile([ROWS, N_HALF], F32, tag="wide")
             y_acc.append(y_bank)
-        for half in range(HALVES):
-            for g in range(TIME_PASSES):
+        for g in range(TIME_PASSES):
+            for half in range(HALVES):
                 cols = slice(half * N_HALF, (half + 1) * N_HALF)
                 nc.tensor.matmul_mx(
                     out=y_acc[half][:],

@@ -26,7 +26,12 @@ CHUNK_K = CHUNK_PASSES * K_PASS
 CHUNKS_PER_MODEL = FEATURES // CHUNK_K
 CHUNKS = MODELS * CHUNKS_PER_MODEL
 BANK_PASSES = 2
-LOADS_AHEAD = 8
+LOAD_CHUNKS_FIRST = (1, 1, 2)
+LOAD_CHUNKS = (2, 2)
+LOAD_CHUNKS_LAST = (2, 1, 1)
+LOAD_CHUNKS_MOST = 2
+LOADS_AHEAD = 5
+BIAS_CHUNK = 2
 
 W_COLS_VECTOR = SAMPLES * 5 // 8
 M_COLS_VECTOR = TIME * 5 // 8
@@ -54,27 +59,35 @@ def tile_model_pb_k_kernel(tc, h_enc, dec_W, dec_b, map_W, map_b, out):
 
         h_raw = {}
         w_raw = {}
+        segments = []
+        for n in range(MODELS):
+            first = n * CHUNKS_PER_MODEL
+            for count in LOAD_CHUNKS_FIRST if n == 0 else LOAD_CHUNKS_LAST if n == MODELS - 1 else LOAD_CHUNKS:
+                segments.append((first, count))
+                first += count
         h_grouped = {}
         w_grouped = {}
         h_mx = {}
         w_mx = {}
         r_acc = {}
 
-        def load_chunk(i):
+        def load_segment(g):
+            i, count = segments[g]
             n, c = divmod(i, CHUNKS_PER_MODEL)
-            features = slice(c * CHUNK_K, (c + 1) * CHUNK_K)
-            h_part = loads.tile([ROWS, CHUNK_K], BF16)
-            nc.sync.dma_start(out=h_part[:], in_=h_rows[n, :, features])
-            h_raw[i] = h_part
-            w_part = loads.tile([P, CHUNK_PASSES, PACK, SAMPLES], BF16)
+            features = slice(c * CHUNK_K, (c + count) * CHUNK_K)
+            h_part = loads.tile([ROWS, LOAD_CHUNKS_MOST * CHUNK_K], BF16)
+            nc.sync.dma_start(out=h_part[:, 0 : count * CHUNK_K], in_=h_rows[n, :, features])
+            w_part = loads.tile([P, LOAD_CHUNKS_MOST * CHUNK_PASSES, PACK, SAMPLES], BF16)
             nc.sync.dma_start(
-                out=w_part[:].rearrange("q c j w -> q c (j w)"),
+                out=w_part[:, 0 : count * CHUNK_PASSES].rearrange("q c j w -> q c (j w)"),
                 in_=dec_W[n, features, :].rearrange("(c q j) w -> q c (j w)", q=P, j=PACK),
             )
-            w_raw[i] = w_part
+            for k in range(count):
+                h_raw[i + k] = h_part[:, k * CHUNK_K : (k + 1) * CHUNK_K]
+                w_raw[i + k] = w_part[:, k * CHUNK_PASSES : (k + 1) * CHUNK_PASSES]
 
         def transpose_h(i):
-            words = h_raw[i][:].bitcast(F32).rearrange("r (c q u) -> r c u q", q=P, u=2)
+            words = h_raw[i].bitcast(F32).rearrange("r (c q u) -> r c u q", q=P, u=2)
             grouped = stage.tile([P, CHUNK_PASSES * ROWS * PACK], BF16, name="h_grouped_sb", align_bytes=64)
             grouped_words = grouped[:].bitcast(F32).rearrange("q (c r u) -> q c r u", c=CHUNK_PASSES, u=2)
             for b in range(CHUNK_PASSES // BANK_PASSES):
@@ -167,6 +180,13 @@ def tile_model_pb_k_kernel(tc, h_enc, dec_W, dec_b, map_W, map_b, out):
                 first = (g * PACK + j) * P
                 nc.tensor.transpose(x_bank[g][:, j, :], x_sb[:, first : first + P], ident_bf16[:])
 
+        def spread_biases():
+            for b in range(2 * TIME // N_HALF):
+                cols = slice(b * N_HALF, (b + 1) * N_HALF)
+                bias_bank = psum_w.tile([P, N_HALF], F32, tag="wide")
+                nc.tensor.matmul(out=bias_bank[:], lhsT=ones[:], rhs=bias_rows[:, cols], start=True, stop=True)
+                nc.scalar.copy(out=bias_sb[:, cols], in_=bias_bank[:])
+
         ident_f32 = keep.tile([P, P], F32)
         make_identity(nc, ident_f32[:])
         ident_bf16 = keep.tile([P, P], BF16)
@@ -176,29 +196,29 @@ def tile_model_pb_k_kernel(tc, h_enc, dec_W, dec_b, map_W, map_b, out):
         nc.vector.memset(bias_rows[:].bitcast(I32), 0)
         ones = keep.tile([P, P], BF16)
         nc.vector.memset(ones[:], 1.0)
-        nc.sync.dma_start(out=bias_rows[0:1, 0:TIME], in_=dec_b.rearrange("n p -> (n p)").unsqueeze(0))
-        nc.sync.dma_start(out=bias_rows[0:1, TIME : 2 * TIME], in_=map_b.unsqueeze(0))
 
         m_raw = keep.tile([P, TIME_PASSES, PACK, TIME], BF16)
         m_grouped = keep.tile([P, TIME_PASSES, TIME, PACK], BF16, align_bytes=64)
         m_words = keep.tile([P, TIME_PASSES, TIME], U32, align_bytes=64)
         m_scales = keep.tile([P, TIME_PASSES, TIME], U8, align_bytes=64)
         load_map(0)
-        for i in range(LOADS_AHEAD):
-            load_chunk(i)
+        load_segment(0)
+        load_segment(1)
+        nc.sync.dma_start(out=bias_rows[0:1, 0:TIME], in_=dec_b.rearrange("n p -> (n p)").unsqueeze(0))
+        nc.sync.dma_start(out=bias_rows[0:1, TIME : 2 * TIME], in_=map_b.unsqueeze(0))
+        for g in range(2, LOADS_AHEAD):
+            load_segment(g)
 
         bias_sb = keep.tile([P, 2 * TIME], F32)
-        for b in range(2 * TIME // N_HALF):
-            cols = slice(b * N_HALF, (b + 1) * N_HALF)
-            bias_bank = psum_w.tile([P, N_HALF], F32, tag="wide")
-            nc.tensor.matmul(out=bias_bank[:], lhsT=ones[:], rhs=bias_rows[:, cols], start=True, stop=True)
-            nc.scalar.copy(out=bias_sb[:, cols], in_=bias_bank[:])
 
         regroup_map(0)
         quantise_map(0)
 
         x_sb = keep.tile([ROWS, TIME], BF16)
+        next_load = LOADS_AHEAD
         for i in range(CHUNKS):
+            if i == BIAS_CHUNK:
+                spread_biases()
             transpose_h(i)
             if i > 0:
                 multiply(i - 1)
@@ -207,8 +227,9 @@ def tile_model_pb_k_kernel(tc, h_enc, dec_W, dec_b, map_W, map_b, out):
             w_mx[i] = quantise(w_grouped[i], "w")
             if i > 0 and i % CHUNKS_PER_MODEL == 0:
                 finish_model(i // CHUNKS_PER_MODEL - 1)
-            if i + LOADS_AHEAD < CHUNKS:
-                load_chunk(i + LOADS_AHEAD)
+            if next_load < len(segments) and i + 1 == sum(segments[next_load - LOADS_AHEAD]):
+                load_segment(next_load)
+                next_load += 1
         load_map(1)
         x_bank = []
         for g in range(TIME_PASSES):

@@ -31,6 +31,7 @@ LOAD_CHUNKS = (2, 2)
 LOAD_CHUNKS_LAST = (2, 1, 1)
 LOAD_CHUNKS_MOST = 2
 LOADS_AHEAD = 5
+MULTIPLY_LAG = 2
 BIAS_CHUNK = 2
 
 W_COLS_VECTOR = SAMPLES * 5 // 8
@@ -220,13 +221,14 @@ def tile_model_pb_k_kernel(tc, h_enc, dec_W, dec_b, map_W, map_b, out):
             if i == BIAS_CHUNK:
                 spread_biases()
             transpose_h(i)
-            if i > 0:
-                multiply(i - 1)
+            if i >= MULTIPLY_LAG:
+                multiply(i - MULTIPLY_LAG)
             regroup_w(i)
             h_mx[i] = quantise(h_grouped[i], "h")
             w_mx[i] = quantise(w_grouped[i], "w")
-            if i > 0 and i % CHUNKS_PER_MODEL == 0:
-                finish_model(i // CHUNKS_PER_MODEL - 1)
+            done = i - MULTIPLY_LAG + 1
+            if done > 0 and done % CHUNKS_PER_MODEL == 0:
+                finish_model(done // CHUNKS_PER_MODEL - 1)
             if next_load < len(segments) and i + 1 == sum(segments[next_load - LOADS_AHEAD]):
                 load_segment(next_load)
                 next_load += 1
@@ -237,7 +239,8 @@ def tile_model_pb_k_kernel(tc, h_enc, dec_W, dec_b, map_W, map_b, out):
             x_bank.append(bank)
         for j in range(PACK - 1):
             transpose_x(j)
-        multiply(CHUNKS - 1)
+        for i in range(CHUNKS - MULTIPLY_LAG, CHUNKS):
+            multiply(i)
         regroup_map(1)
         finish_model(MODELS - 1)
         transpose_x(PACK - 1)

@@ -113,8 +113,8 @@ def tile_model_pb_k_kernel(tc, h_enc, dec_W, dec_b, map_W, map_b, out):
                 in_=w_raw[i][:, :, :, 0:W_COLS_VECTOR].rearrange("q c j (g i) -> q c g j i", i=4),
             )
             nc.scalar.copy(
-                out=grouped[:, :, W_COLS_VECTOR:SAMPLES, :],
-                in_=w_raw[i][:, :, :, W_COLS_VECTOR:SAMPLES].rearrange("q c j w -> q c w j"),
+                out=grouped[:, :, W_COLS_VECTOR:SAMPLES, :].rearrange("q c (g i) j -> q c g j i", i=4),
+                in_=w_raw[i][:, :, :, W_COLS_VECTOR:SAMPLES].rearrange("q c j (g i) -> q c g j i", i=4),
             )
             w_grouped[i] = grouped[:].rearrange("q c w j -> q (c w j)")
 
@@ -163,8 +163,8 @@ def tile_model_pb_k_kernel(tc, h_enc, dec_W, dec_b, map_W, map_b, out):
                 in_=m_raw[:, g, :, 0:M_COLS_VECTOR].rearrange("q j (c i) -> q c j i", i=4),
             )
             nc.scalar.copy(
-                out=m_grouped[:, g, M_COLS_VECTOR:TIME, :],
-                in_=m_raw[:, g, :, M_COLS_VECTOR:TIME].rearrange("q j s -> q s j"),
+                out=m_grouped[:, g, M_COLS_VECTOR:TIME, :].rearrange("q (c i) j -> q c j i", i=4),
+                in_=m_raw[:, g, :, M_COLS_VECTOR:TIME].rearrange("q j (c i) -> q c j i", i=4),
             )
 
         def quantise_map(g):

@@ -20,22 +20,29 @@ ROWS = 128
 FEATURES = 8192
 SAMPLES = 128
 TIME = MODELS * SAMPLES
+PASSES = FEATURES // K_PASS
 
-CHUNK_PASSES = 4
-CHUNK_K = CHUNK_PASSES * K_PASS
-CHUNKS_PER_MODEL = FEATURES // CHUNK_K
-CHUNKS = MODELS * CHUNKS_PER_MODEL
-BANK_PASSES = 2
-LOAD_CHUNKS_FIRST = (1, 1, 2)
-LOAD_CHUNKS = (2, 2)
-LOAD_CHUNKS_LAST = (2, 1, 1)
-LOAD_CHUNKS_MOST = 2
-LOADS_AHEAD = 5
+STEP_PASSES_FIRST = (2, 2, 4, 4, 4)
+STEP_PASSES = (4, 4, 4, 4)
+STEP_PASSES_LAST = (4, 4, 4, 2, 2)
+STEP_MOST = 4
+LOAD_PASSES_FIRST = (2,2,4,4,4)
+LOAD_PASSES = (8, 8)
+LOAD_PASSES_LAST = (4,4,4,2,2)
+LOAD_MOST = 8
 MULTIPLY_LAG = 2
-BIAS_CHUNK = 2
+BANK_PASSES = 2
+STAGE_BUFS = 4
+LOADS_AHEAD = 4
+LOAD_BUFS = LOADS_AHEAD + 1
+
+BIAS_STEP = 2
+MAP_PARTS = ((0, 0, 1024), (1, 0, 512), (1, 512, 1024))
+MAP_LOADS = (1, 2)
+MAP_STEPS = (1, 2)
+LAST_MAP_PART = 2
 
 W_COLS_VECTOR = SAMPLES * 5 // 8
-M_COLS_VECTOR = TIME * 5 // 8
 
 TIME_PASSES = TIME // K_PASS
 N_HALF = 512
@@ -51,87 +58,99 @@ def tile_model_pb_k_kernel(tc, h_enc, dec_W, dec_b, map_W, map_b, out):
 
     with ExitStack() as ctx:
         keep = ctx.enter_context(tc.tile_pool(name="keep", bufs=1))
-        loads = ctx.enter_context(tc.tile_pool(name="loads", bufs=LOADS_AHEAD))
-        stage = ctx.enter_context(tc.tile_pool(name="stage", bufs=4))
+        loads = ctx.enter_context(tc.tile_pool(name="loads", bufs=LOAD_BUFS))
+        stage = ctx.enter_context(tc.tile_pool(name="stage", bufs=STAGE_BUFS))
         psum_t = ctx.enter_context(tc.psum_pool(name="psum_t", bufs=4))
         psum_r = ctx.enter_context(tc.psum_pool(name="psum_r", bufs=2))
         psum_w = ctx.enter_context(tc.psum_pool(name="psum_w", bufs=2))
         ctx.enter_context(tc.manual_schedule())
 
+        def cut(of_first, of_others, of_last):
+            pieces = []
+            for n in range(MODELS):
+                first = 0
+                for count in of_first if n == 0 else of_last if n == MODELS - 1 else of_others:
+                    pieces.append((n, first, count))
+                    first += count
+            return pieces
+
+        steps = cut(STEP_PASSES_FIRST, STEP_PASSES, STEP_PASSES_LAST)
+        load_pieces = cut(LOAD_PASSES_FIRST, LOAD_PASSES, LOAD_PASSES_LAST)
+
         h_raw = {}
         w_raw = {}
-        segments = []
-        for n in range(MODELS):
-            first = n * CHUNKS_PER_MODEL
-            for count in LOAD_CHUNKS_FIRST if n == 0 else LOAD_CHUNKS_LAST if n == MODELS - 1 else LOAD_CHUNKS:
-                segments.append((first, count))
-                first += count
         h_grouped = {}
         w_grouped = {}
         h_mx = {}
         w_mx = {}
         r_acc = {}
 
-        def load_segment(g):
-            i, count = segments[g]
-            n, c = divmod(i, CHUNKS_PER_MODEL)
-            features = slice(c * CHUNK_K, (c + count) * CHUNK_K)
-            h_part = loads.tile([ROWS, LOAD_CHUNKS_MOST * CHUNK_K], BF16)
-            nc.sync.dma_start(out=h_part[:, 0 : count * CHUNK_K], in_=h_rows[n, :, features])
-            w_part = loads.tile([P, LOAD_CHUNKS_MOST * CHUNK_PASSES, PACK, SAMPLES], BF16)
+        def load(piece):
+            if piece in MAP_LOADS:
+                load_map(MAP_LOADS.index(piece))
+            n, first, count = load_pieces[piece]
+            features = slice(first * K_PASS, (first + count) * K_PASS)
+            h_part = loads.tile([ROWS, LOAD_MOST, K_PASS], BF16)
             nc.sync.dma_start(
-                out=w_part[:, 0 : count * CHUNK_PASSES].rearrange("q c j w -> q c (j w)"),
+                out=h_part[:, 0:count].rearrange("r c k -> r (c k)"),
+                in_=h_rows[n, :, features],
+            )
+            w_part = loads.tile([P, LOAD_MOST, PACK, SAMPLES], BF16)
+            nc.sync.dma_start(
+                out=w_part[:, 0:count].rearrange("q c j w -> q c (j w)"),
                 in_=dec_W[n, features, :].rearrange("(c q j) w -> q c (j w)", q=P, j=PACK),
             )
-            for k in range(count):
-                h_raw[i + k] = h_part[:, k * CHUNK_K : (k + 1) * CHUNK_K]
-                w_raw[i + k] = w_part[:, k * CHUNK_PASSES : (k + 1) * CHUNK_PASSES]
+            for c in range(count):
+                h_raw[n, first + c] = (h_part, c)
+                w_raw[n, first + c] = (w_part, c)
 
         def transpose_h(i):
-            words = h_raw[i].bitcast(F32).rearrange("r (c q u) -> r c u q", q=P, u=2)
-            grouped = stage.tile([P, CHUNK_PASSES * ROWS * PACK], BF16, name="h_grouped_sb", align_bytes=64)
-            grouped_words = grouped[:].bitcast(F32).rearrange("q (c r u) -> q c r u", c=CHUNK_PASSES, u=2)
-            for b in range(CHUNK_PASSES // BANK_PASSES):
+            n, first_pass, count = steps[i]
+            part, place = h_raw[n, first_pass]
+            words = part[:, place : place + count].bitcast(F32).rearrange("r c (q u) -> r c u q", u=2)
+            grouped = stage.tile([P, STEP_MOST * ROWS * PACK], BF16, name="h_grouped_sb", align_bytes=64)
+            grouped_words = grouped[:].bitcast(F32).rearrange("q (c r u) -> q c r u", c=STEP_MOST, u=2)
+            for first in range(0, count, BANK_PASSES):
                 bank = psum_t.tile([P, BANK_PASSES, 2, ROWS], F32, name="h_bank")
                 for cb in range(BANK_PASSES):
                     for u in range(2):
-                        nc.tensor.transpose(
-                            bank[:, cb, u, :],
-                            words[:, b * BANK_PASSES + cb, u, :],
-                            ident_f32[:],
-                        )
+                        nc.tensor.transpose(bank[:, cb, u, :], words[:, first + cb, u, :], ident_f32[:])
                 nc.scalar.copy(
-                    out=grouped_words[:, b * BANK_PASSES : (b + 1) * BANK_PASSES],
+                    out=grouped_words[:, first : first + BANK_PASSES],
                     in_=bank[:].rearrange("q c u r -> q c r u"),
                 )
-            h_grouped[i] = grouped[:]
+            h_grouped[i] = grouped[:, 0 : count * ROWS * PACK]
 
         def regroup_w(i):
-            grouped = stage.tile([P, CHUNK_PASSES, SAMPLES, PACK], BF16, name="w_grouped_sb", align_bytes=64)
+            n, first_pass, count = steps[i]
+            part, place = w_raw[n, first_pass]
+            raw = part[:, place : place + count]
+            grouped = stage.tile([P, STEP_MOST, SAMPLES, PACK], BF16, name="w_grouped_sb", align_bytes=64)
             nc.vector.tensor_copy(
-                out=grouped[:, :, 0:W_COLS_VECTOR, :].rearrange("q c (g i) j -> q c g j i", i=4),
-                in_=w_raw[i][:, :, :, 0:W_COLS_VECTOR].rearrange("q c j (g i) -> q c g j i", i=4),
+                out=grouped[:, 0:count, 0:W_COLS_VECTOR, :].rearrange("q c (g i) j -> q c g j i", i=4),
+                in_=raw[:, :, :, 0:W_COLS_VECTOR].rearrange("q c j (g i) -> q c g j i", i=4),
             )
             nc.scalar.copy(
-                out=grouped[:, :, W_COLS_VECTOR:SAMPLES, :].rearrange("q c (g i) j -> q c g j i", i=4),
-                in_=w_raw[i][:, :, :, W_COLS_VECTOR:SAMPLES].rearrange("q c j (g i) -> q c g j i", i=4),
+                out=grouped[:, 0:count, W_COLS_VECTOR:SAMPLES, :].rearrange("q c (g i) j -> q c g j i", i=4),
+                in_=raw[:, :, :, W_COLS_VECTOR:SAMPLES].rearrange("q c j (g i) -> q c g j i", i=4),
             )
-            w_grouped[i] = grouped[:].rearrange("q c w j -> q (c w j)")
+            w_grouped[i] = grouped[:, 0:count].rearrange("q c w j -> q (c w j)")
 
-        def quantise(values, operand):
-            words = stage.tile([P, CHUNK_PASSES * P], U32, tag=operand + "_words", align_bytes=64)
-            scales = stage.tile([P, CHUNK_PASSES * P], U8, tag=operand + "_scales", align_bytes=64)
-            nc.vector.quantize_mx(out=words[:].bitcast(FP8X4), scales=scales[:], in_=values)
+        def quantise(i, values, operand):
+            width = steps[i][2] * P
+            words = stage.tile([P, STEP_MOST * P], U32, tag=operand + "_words", align_bytes=64)
+            scales = stage.tile([P, STEP_MOST * P], U8, tag=operand + "_scales", align_bytes=64)
+            nc.vector.quantize_mx(out=words[:, 0:width].bitcast(FP8X4), scales=scales[:, 0:width], in_=values)
             return words, scales
 
         def multiply(i):
-            n, c = divmod(i, CHUNKS_PER_MODEL)
-            if c == 0:
+            n, first, count = steps[i]
+            if first == 0:
                 acc = psum_r.tile([ROWS, SAMPLES], F32, name="r_sums")
                 r_acc[n] = acc
             h_words, h_scales = h_mx[i]
             w_words, w_scales = w_mx[i]
-            for cp in range(CHUNK_PASSES):
+            for cp in range(count):
                 cols = slice(cp * P, (cp + 1) * P)
                 nc.tensor.matmul_mx(
                     out=r_acc[n][:],
@@ -139,8 +158,8 @@ def tile_model_pb_k_kernel(tc, h_enc, dec_W, dec_b, map_W, map_b, out):
                     lhsT_scale=h_scales[:, cols],
                     rhs=w_words[:, cols].bitcast(FP8X4),
                     rhs_scale=w_scales[:, cols],
-                    start=(c == 0 and cp == 0),
-                    stop=(c == CHUNKS_PER_MODEL - 1 and cp == CHUNK_PASSES - 1),
+                    start=(first + cp == 0),
+                    stop=(first + cp == PASSES - 1),
                 )
 
         def finish_model(n):
@@ -151,30 +170,32 @@ def tile_model_pb_k_kernel(tc, h_enc, dec_W, dec_b, map_W, map_b, out):
                 op=ADD,
             )
 
-        def load_map(g):
+        def load_map(part):
+            g, first, end = MAP_PARTS[part]
             nc.sync.dma_start(
-                out=m_raw[:, g],
-                in_=map_W[g * K_PASS : (g + 1) * K_PASS, :].rearrange("(q j) s -> q j s", j=PACK),
+                out=m_raw[:, g, :, first:end],
+                in_=map_W[g * K_PASS : (g + 1) * K_PASS, first:end].rearrange("(q j) s -> q j s", j=PACK),
             )
 
-        def regroup_map(g):
+        def regroup_map(part):
+            g, first, end = MAP_PARTS[part]
+            split = first + (end - first) * 5 // 8
             nc.vector.tensor_copy(
-                out=m_grouped[:, g, 0:M_COLS_VECTOR, :].rearrange("q (c i) j -> q c j i", i=4),
-                in_=m_raw[:, g, :, 0:M_COLS_VECTOR].rearrange("q j (c i) -> q c j i", i=4),
+                out=m_grouped[:, g, first:split, :].rearrange("q (c i) j -> q c j i", i=4),
+                in_=m_raw[:, g, :, first:split].rearrange("q j (c i) -> q c j i", i=4),
             )
             nc.scalar.copy(
-                out=m_grouped[:, g, M_COLS_VECTOR:TIME, :].rearrange("q (c i) j -> q c j i", i=4),
-                in_=m_raw[:, g, :, M_COLS_VECTOR:TIME].rearrange("q j (c i) -> q c j i", i=4),
+                out=m_grouped[:, g, split:end, :].rearrange("q (c i) j -> q c j i", i=4),
+                in_=m_raw[:, g, :, split:end].rearrange("q j (c i) -> q c j i", i=4),
             )
 
-        def quantise_map(g):
-            for half in range(HALVES):
-                cols = slice(half * N_HALF, (half + 1) * N_HALF)
-                nc.vector.quantize_mx(
-                    out=m_words[:, g, cols].bitcast(FP8X4),
-                    scales=m_scales[:, g, cols],
-                    in_=m_grouped[:, g, cols, :].rearrange("q s j -> q (s j)"),
-                )
+        def quantise_map(part):
+            g, first, end = MAP_PARTS[part]
+            nc.vector.quantize_mx(
+                out=m_words[:, g, first:end].bitcast(FP8X4),
+                scales=m_scales[:, g, first:end],
+                in_=m_grouped[:, g, first:end].rearrange("q s j -> q (s j)"),
+            )
 
         def transpose_x(j):
             for g in range(TIME_PASSES):
@@ -182,87 +203,95 @@ def tile_model_pb_k_kernel(tc, h_enc, dec_W, dec_b, map_W, map_b, out):
                 nc.tensor.transpose(x_bank[g][:, j, :], x_sb[:, first : first + P], ident_bf16[:])
 
         def spread_biases():
-            for b in range(2 * TIME // N_HALF):
-                cols = slice(b * N_HALF, (b + 1) * N_HALF)
-                bias_bank = psum_w.tile([P, N_HALF], F32, tag="wide")
-                nc.tensor.matmul(out=bias_bank[:], lhsT=ones[:], rhs=bias_rows[:, cols], start=True, stop=True)
-                nc.scalar.copy(out=bias_sb[:, cols], in_=bias_bank[:])
-
-        ident_f32 = keep.tile([P, P], F32)
-        make_identity(nc, ident_f32[:])
-        ident_bf16 = keep.tile([P, P], BF16)
-        make_identity(nc, ident_bf16[:])
-
-        bias_rows = keep.tile([P, 2 * TIME], BF16)
-        nc.vector.memset(bias_rows[:].bitcast(I32), 0)
-        ones = keep.tile([P, P], BF16)
-        nc.vector.memset(ones[:], 1.0)
+            for b in range(2):
+                bias_bank = psum_w.tile([P, TIME], BF16, tag="wide")
+                for half in range(HALVES):
+                    cols = slice(half * N_HALF, (half + 1) * N_HALF)
+                    nc.tensor.matmul(
+                        out=bias_bank[:, cols],
+                        lhsT=ones[:],
+                        rhs=bias_rows[:, b * TIME + half * N_HALF : b * TIME + (half + 1) * N_HALF],
+                        start=True,
+                        stop=True,
+                    )
+                nc.scalar.copy(out=bias_sb[:, b * TIME : (b + 1) * TIME], in_=bias_bank[:])
 
         m_raw = keep.tile([P, TIME_PASSES, PACK, TIME], BF16)
         m_grouped = keep.tile([P, TIME_PASSES, TIME, PACK], BF16, align_bytes=64)
         m_words = keep.tile([P, TIME_PASSES, TIME], U32, align_bytes=64)
         m_scales = keep.tile([P, TIME_PASSES, TIME], U8, align_bytes=64)
-        load_map(0)
-        load_segment(0)
-        load_segment(1)
+        bias_rows = keep.tile([P, 2 * TIME], BF16)
+        nc.vector.memset(bias_rows[:].bitcast(I32), 0)
+        ones = keep.tile([P, P], BF16)
+        nc.vector.memset(ones[:], 1.0)
+        load(0)
+        load(1)
         nc.sync.dma_start(out=bias_rows[0:1, 0:TIME], in_=dec_b.rearrange("n p -> (n p)").unsqueeze(0))
         nc.sync.dma_start(out=bias_rows[0:1, TIME : 2 * TIME], in_=map_b.unsqueeze(0))
-        for g in range(2, LOADS_AHEAD):
-            load_segment(g)
+        for piece in range(2, LOADS_AHEAD):
+            load(piece)
 
-        bias_sb = keep.tile([P, 2 * TIME], F32)
-
-        regroup_map(0)
-        quantise_map(0)
+        ident_f32 = keep.tile([P, P], F32)
+        make_identity(nc, ident_f32[:])
+        ident_bf16 = keep.tile([P, P], BF16)
+        make_identity(nc, ident_bf16[:])
+        bias_sb = keep.tile([P, 2 * TIME], BF16)
 
         x_sb = keep.tile([ROWS, TIME], BF16)
         next_load = LOADS_AHEAD
-        for i in range(CHUNKS):
-            if i == BIAS_CHUNK:
+        for i in range(len(steps)):
+            if i == BIAS_STEP:
                 spread_biases()
+            if i in MAP_STEPS:
+                regroup_map(MAP_STEPS.index(i))
             transpose_h(i)
             if i >= MULTIPLY_LAG:
                 multiply(i - MULTIPLY_LAG)
             regroup_w(i)
-            h_mx[i] = quantise(h_grouped[i], "h")
-            w_mx[i] = quantise(w_grouped[i], "w")
-            done = i - MULTIPLY_LAG + 1
-            if done > 0 and done % CHUNKS_PER_MODEL == 0:
-                finish_model(done // CHUNKS_PER_MODEL - 1)
-            if next_load < len(segments) and i + 1 == sum(segments[next_load - LOADS_AHEAD]):
-                load_segment(next_load)
-                next_load += 1
-        load_map(1)
+            if i in MAP_STEPS:
+                quantise_map(MAP_STEPS.index(i))
+            h_mx[i] = quantise(i, h_grouped[i], "h")
+            w_mx[i] = quantise(i, w_grouped[i], "w")
+            if i >= MULTIPLY_LAG:
+                n, first, count = steps[i - MULTIPLY_LAG]
+                if first + count == PASSES:
+                    finish_model(n)
+            if next_load < len(load_pieces):
+                n, first, count = load_pieces[next_load - LOADS_AHEAD]
+                if steps[i][0] == n and steps[i][1] + steps[i][2] == first + count:
+                    load(next_load)
+                    next_load += 1
+        load_map(LAST_MAP_PART)
         x_bank = []
         for g in range(TIME_PASSES):
             bank = psum_w.tile([P, PACK, ROWS], BF16, tag="wide")
             x_bank.append(bank)
         for j in range(PACK - 1):
             transpose_x(j)
-        for i in range(CHUNKS - MULTIPLY_LAG, CHUNKS):
+        for i in range(len(steps) - MULTIPLY_LAG, len(steps)):
             multiply(i)
-        regroup_map(1)
         finish_model(MODELS - 1)
+        regroup_map(LAST_MAP_PART)
         transpose_x(PACK - 1)
 
         x_grouped = keep.tile([P, TIME_PASSES, ROWS, PACK], BF16, align_bytes=64)
         x_words = keep.tile([P, TIME_PASSES, ROWS], U32, align_bytes=64)
         x_scales = keep.tile([P, TIME_PASSES, ROWS], U8, align_bytes=64)
-        nc.vector.tensor_copy(out=x_grouped[:, 0], in_=x_bank[0][:].rearrange("q j r -> q r j"))
-        nc.scalar.copy(out=x_grouped[:, 1], in_=x_bank[1][:].rearrange("q j r -> q r j"))
+        for g in range(TIME_PASSES):
+            nc.scalar.copy(out=x_grouped[:, g], in_=x_bank[g][:].rearrange("q j r -> q r j"))
         for g in range(TIME_PASSES):
             nc.vector.quantize_mx(
                 out=x_words[:, g].bitcast(FP8X4),
                 scales=x_scales[:, g],
                 in_=x_grouped[:, g].rearrange("q r j -> q (r j)"),
             )
-        quantise_map(1)
+        quantise_map(LAST_MAP_PART)
         y_acc = []
         for half in range(HALVES):
             y_bank = psum_w.tile([ROWS, N_HALF], F32, tag="wide")
             y_acc.append(y_bank)
-        for g in range(TIME_PASSES):
-            for half in range(HALVES):
+        for half in range(HALVES):
+            for g in range(TIME_PASSES):
                 cols = slice(half * N_HALF, (half + 1) * N_HALF)
                 nc.tensor.matmul_mx(
                     out=y_acc[half][:],

@@ -22,13 +22,9 @@ SAMPLES = 128
 TIME = MODELS * SAMPLES
 PASSES = FEATURES // K_PASS
 
-STEP_PASSES_FIRST = (2, 2, 4, 4, 4)
-STEP_PASSES = (4, 4, 4, 4)
-STEP_PASSES_LAST = (4, 4, 4, 2, 2)
+STEP_PASSES = [(4, 4, 4, 4)] * (MODELS - 1) + [(4, 4, 4, 2, 2)]
+LOAD_PASSES = [(4, 4, 8)] + [(8, 8)] * (MODELS - 3) + [(8, 4, 4)] + [(4, 4, 4, 2, 2)]
 STEP_MOST = 4
-LOAD_PASSES_FIRST = (2,2,4,4,4)
-LOAD_PASSES = (8, 8)
-LOAD_PASSES_LAST = (4,4,4,2,2)
 LOAD_MOST = 8
 MULTIPLY_LAG = 2
 BANK_PASSES = 2
@@ -37,12 +33,14 @@ LOADS_AHEAD = 4
 LOAD_BUFS = LOADS_AHEAD + 1
 
 BIAS_STEP = 2
-MAP_PARTS = ((0, 0, 1024), (1, 0, 512), (1, 512, 1024))
+MAP_EARLY = ((0, 0), (1, 0))
 MAP_LOADS = (1, 2)
 MAP_STEPS = (1, 2)
-LAST_MAP_PART = 2
+MAP_LATE = ((0, 1), (1, 1))
 
-W_COLS_VECTOR = SAMPLES * 5 // 8
+W_COLS_VECTOR = SAMPLES * 21 // 32
+M_COLS_VECTOR = 512 * 5 // 8
+OUT_PIECES = ((0, 0, 512), (1, 0, 256), (1, 256, 512))
 
 TIME_PASSES = TIME // K_PASS
 N_HALF = 512
@@ -65,17 +63,17 @@ def tile_model_pb_k_kernel(tc, h_enc, dec_W, dec_b, map_W, map_b, out):
         psum_w = ctx.enter_context(tc.psum_pool(name="psum_w", bufs=2))
         ctx.enter_context(tc.manual_schedule())
 
-        def cut(of_first, of_others, of_last):
+        def cut(of_model):
             pieces = []
             for n in range(MODELS):
                 first = 0
-                for count in of_first if n == 0 else of_last if n == MODELS - 1 else of_others:
+                for count in of_model[n]:
                     pieces.append((n, first, count))
                     first += count
             return pieces
 
-        steps = cut(STEP_PASSES_FIRST, STEP_PASSES, STEP_PASSES_LAST)
-        load_pieces = cut(LOAD_PASSES_FIRST, LOAD_PASSES, LOAD_PASSES_LAST)
+        steps = cut(STEP_PASSES)
+        load_pieces = cut(LOAD_PASSES)
 
         h_raw = {}
         w_raw = {}
@@ -87,7 +85,7 @@ def tile_model_pb_k_kernel(tc, h_enc, dec_W, dec_b, map_W, map_b, out):
 
         def load(piece):
             if piece in MAP_LOADS:
-                load_map(MAP_LOADS.index(piece))
+                load_map(MAP_EARLY[MAP_LOADS.index(piece)])
             n, first, count = load_pieces[piece]
             features = slice(first * K_PASS, (first + count) * K_PASS)
             h_part = loads.tile([ROWS, LOAD_MOST, K_PASS], BF16)
@@ -171,30 +169,31 @@ def tile_model_pb_k_kernel(tc, h_enc, dec_W, dec_b, map_W, map_b, out):
             )
 
         def load_map(part):
-            g, first, end = MAP_PARTS[part]
+            g, half = part
             nc.sync.dma_start(
-                out=m_raw[:, g, :, first:end],
-                in_=map_W[g * K_PASS : (g + 1) * K_PASS, first:end].rearrange("(q j) s -> q j s", j=PACK),
+                out=m_raw[:, g, half],
+                in_=map_W[g * K_PASS : (g + 1) * K_PASS, half * N_HALF : (half + 1) * N_HALF].rearrange(
+                    "(q j) s -> q j s", j=PACK
+                ),
             )
 
         def regroup_map(part):
-            g, first, end = MAP_PARTS[part]
-            split = first + (end - first) * 5 // 8
+            g, half = part
             nc.vector.tensor_copy(
-                out=m_grouped[:, g, first:split, :].rearrange("q (c i) j -> q c j i", i=4),
-                in_=m_raw[:, g, :, first:split].rearrange("q j (c i) -> q c j i", i=4),
+                out=m_grouped[:, g, half, 0:M_COLS_VECTOR, :].rearrange("q (c i) j -> q c j i", i=4),
+                in_=m_raw[:, g, half, :, 0:M_COLS_VECTOR].rearrange("q j (c i) -> q c j i", i=4),
             )
             nc.scalar.copy(
-                out=m_grouped[:, g, split:end, :].rearrange("q (c i) j -> q c j i", i=4),
-                in_=m_raw[:, g, :, split:end].rearrange("q j (c i) -> q c j i", i=4),
+                out=m_grouped[:, g, half, M_COLS_VECTOR:N_HALF, :].rearrange("q (c i) j -> q c j i", i=4),
+                in_=m_raw[:, g, half, :, M_COLS_VECTOR:N_HALF].rearrange("q j (c i) -> q c j i", i=4),
             )
 
         def quantise_map(part):
-            g, first, end = MAP_PARTS[part]
+            g, half = part
             nc.vector.quantize_mx(
-                out=m_words[:, g, first:end].bitcast(FP8X4),
-                scales=m_scales[:, g, first:end],
-                in_=m_grouped[:, g, first:end].rearrange("q s j -> q (s j)"),
+                out=m_words[:, g, half].bitcast(FP8X4),
+                scales=m_scales[:, g, half],
+                in_=m_grouped[:, g, half].rearrange("q s j -> q (s j)"),
             )
 
         def transpose_x(j):
@@ -216,10 +215,10 @@ def tile_model_pb_k_kernel(tc, h_enc, dec_W, dec_b, map_W, map_b, out):
                     )
                 nc.scalar.copy(out=bias_sb[:, b * TIME : (b + 1) * TIME], in_=bias_bank[:])
 
-        m_raw = keep.tile([P, TIME_PASSES, PACK, TIME], BF16)
-        m_grouped = keep.tile([P, TIME_PASSES, TIME, PACK], BF16, align_bytes=64)
-        m_words = keep.tile([P, TIME_PASSES, TIME], U32, align_bytes=64)
-        m_scales = keep.tile([P, TIME_PASSES, TIME], U8, align_bytes=64)
+        m_raw = keep.tile([P, TIME_PASSES, HALVES, PACK, N_HALF], BF16)
+        m_grouped = keep.tile([P, TIME_PASSES, HALVES, N_HALF, PACK], BF16, align_bytes=64)
+        m_words = keep.tile([P, TIME_PASSES, HALVES, N_HALF], U32, align_bytes=64)
+        m_scales = keep.tile([P, TIME_PASSES, HALVES, N_HALF], U8, align_bytes=64)
         bias_rows = keep.tile([P, 2 * TIME], BF16)
         nc.vector.memset(bias_rows[:].bitcast(I32), 0)
         ones = keep.tile([P, P], BF16)
@@ -243,13 +242,13 @@ def tile_model_pb_k_kernel(tc, h_enc, dec_W, dec_b, map_W, map_b, out):
             if i == BIAS_STEP:
                 spread_biases()
             if i in MAP_STEPS:
-                regroup_map(MAP_STEPS.index(i))
+                regroup_map(MAP_EARLY[MAP_STEPS.index(i)])
             transpose_h(i)
             if i >= MULTIPLY_LAG:
                 multiply(i - MULTIPLY_LAG)
             regroup_w(i)
             if i in MAP_STEPS:
-                quantise_map(MAP_STEPS.index(i))
+                quantise_map(MAP_EARLY[MAP_STEPS.index(i)])
             h_mx[i] = quantise(i, h_grouped[i], "h")
             w_mx[i] = quantise(i, w_grouped[i], "w")
             if i >= MULTIPLY_LAG:
@@ -261,7 +260,8 @@ def tile_model_pb_k_kernel(tc, h_enc, dec_W, dec_b, map_W, map_b, out):
                 if steps[i][0] == n and steps[i][1] + steps[i][2] == first + count:
                     load(next_load)
                     next_load += 1
-        load_map(LAST_MAP_PART)
+        for part in MAP_LATE:
+            load_map(part)
         x_bank = []
         for g in range(TIME_PASSES):
             bank = psum_w.tile([P, PACK, ROWS], BF16, tag="wide")
@@ -271,41 +271,44 @@ def tile_model_pb_k_kernel(tc, h_enc, dec_W, dec_b, map_W, map_b, out):
         for i in range(len(steps) - MULTIPLY_LAG, len(steps)):
             multiply(i)
         finish_model(MODELS - 1)
-        regroup_map(LAST_MAP_PART)
         transpose_x(PACK - 1)
+        regroup_map(MAP_LATE[0])
 
         x_grouped = keep.tile([P, TIME_PASSES, ROWS, PACK], BF16, align_bytes=64)
         x_words = keep.tile([P, TIME_PASSES, ROWS], U32, align_bytes=64)
         x_scales = keep.tile([P, TIME_PASSES, ROWS], U8, align_bytes=64)
         for g in range(TIME_PASSES):
             nc.scalar.copy(out=x_grouped[:, g], in_=x_bank[g][:].rearrange("q j r -> q r j"))
+        regroup_map(MAP_LATE[1])
         for g in range(TIME_PASSES):
             nc.vector.quantize_mx(
                 out=x_words[:, g].bitcast(FP8X4),
                 scales=x_scales[:, g],
                 in_=x_grouped[:, g].rearrange("q r j -> q (r j)"),
             )
-        quantise_map(LAST_MAP_PART)
+        for part in MAP_LATE:
+            quantise_map(part)
         y_acc = []
         for half in range(HALVES):
             y_bank = psum_w.tile([ROWS, N_HALF], F32, tag="wide")
             y_acc.append(y_bank)
         for half in range(HALVES):
             for g in range(TIME_PASSES):
-                cols = slice(half * N_HALF, (half + 1) * N_HALF)
                 nc.tensor.matmul_mx(
                     out=y_acc[half][:],
                     lhsT=x_words[:, g].bitcast(FP8X4),
                     lhsT_scale=x_scales[:, g],
-                    rhs=m_words[:, g, cols].bitcast(FP8X4),
-                    rhs_scale=m_scales[:, g, cols],
+                    rhs=m_words[:, g, half].bitcast(FP8X4),
+                    rhs_scale=m_scales[:, g, half],
                     start=(g == 0),
                     stop=(g == TIME_PASSES - 1),
                 )
-        for half in range(HALVES):
-            cols = slice(half * N_HALF, (half + 1) * N_HALF)
+        for half, first, end in OUT_PIECES:
             y_sb = stage.tile([ROWS, N_HALF], F32)
             nc.vector.tensor_tensor(
-                out=y_sb[:], in0=y_acc[half][:], in1=bias_sb[:, TIME + half * N_HALF : TIME + (half + 1) * N_HALF], op=ADD
+                out=y_sb[:, 0 : end - first],
+                in0=y_acc[half][:, first:end],
+                in1=bias_sb[:, TIME + half * N_HALF + first : TIME + half * N_HALF + end],
+                op=ADD,
             )
-            nc.sync.dma_start(out=out_rows[:, cols], in_=y_sb[:])
+            nc.sync.dma_start(out=out_rows[:, half * N_HALF + first : half * N_HALF + end], in_=y_sb[:, 0 : end - first])

@@ -39,7 +39,7 @@ MAP_STEPS = (1, 2)
 MAP_LATE = ((0, 1), (1, 1))
 
 W_COLS_VECTOR = SAMPLES * 21 // 32
-M_COLS_VECTOR = 512 * 5 // 8
+M_COLS_VECTOR = 512 * 9 // 16
 OUT_PIECES = ((0, 0, 512), (1, 0, 256), (1, 256, 512))
 
 TIME_PASSES = TIME // K_PASS
@@ -270,24 +270,24 @@ def tile_model_pb_k_kernel(tc, h_enc, dec_W, dec_b, map_W, map_b, out):
             transpose_x(j)
         for i in range(len(steps) - MULTIPLY_LAG, len(steps)):
             multiply(i)
+        regroup_map(MAP_LATE[0])
         finish_model(MODELS - 1)
         transpose_x(PACK - 1)
-        regroup_map(MAP_LATE[0])
+        regroup_map(MAP_LATE[1])
 
         x_grouped = keep.tile([P, TIME_PASSES, ROWS, PACK], BF16, align_bytes=64)
         x_words = keep.tile([P, TIME_PASSES, ROWS], U32, align_bytes=64)
         x_scales = keep.tile([P, TIME_PASSES, ROWS], U8, align_bytes=64)
         for g in range(TIME_PASSES):
             nc.scalar.copy(out=x_grouped[:, g], in_=x_bank[g][:].rearrange("q j r -> q r j"))
-        regroup_map(MAP_LATE[1])
+        quantise_map(MAP_LATE[0])
         for g in range(TIME_PASSES):
             nc.vector.quantize_mx(
                 out=x_words[:, g].bitcast(FP8X4),
                 scales=x_scales[:, g],
                 in_=x_grouped[:, g].rearrange("q r j -> q (r j)"),
             )
-        for part in MAP_LATE:
-            quantise_map(part)
+        quantise_map(MAP_LATE[1])
         y_acc = []
         for half in range(HALVES):
             y_bank = psum_w.tile([ROWS, N_HALF], F32, tag="wide")

from contextlib import ExitStack

import concourse.mybir as mybir
from concourse.masks import make_identity

BF16 = mybir.dt.bfloat16
F32 = mybir.dt.float32
I32 = mybir.dt.int32
U32 = mybir.dt.uint32
U8 = mybir.dt.uint8
FP8X4 = mybir.dt.float8_e4m3fn_x4
ADD = mybir.AluOpType.add

P = 128
PACK = 4
K_PASS = P * PACK

MODELS = 8
ROWS = 128
FEATURES = 8192
SAMPLES = 128
TIME = MODELS * SAMPLES
PASSES = FEATURES // K_PASS

STEP_PASSES = [(4, 4, 4, 4)] * (MODELS - 1) + [(4, 4, 4, 2, 2)]
LOAD_PASSES = [(4, 4, 8)] + [(8, 8)] * (MODELS - 3) + [(8, 4, 4)] + [(4, 4, 4, 2, 2)]
STEP_MOST = 4
LOAD_MOST = 8
MULTIPLY_LAG = 2
BANK_PASSES = 2
STAGE_BUFS = 4
LOADS_AHEAD = 4
LOAD_BUFS = LOADS_AHEAD + 1

BIAS_STEP = 2
MAP_EARLY = ((0, 0), (1, 0))
MAP_LOADS = (1, 2)
MAP_STEPS = (1, 2)
MAP_LATE = ((0, 1), (1, 1))

W_COLS_VECTOR = SAMPLES * 21 // 32
M_COLS_VECTOR = 512 * 9 // 16
OUT_PIECES = ((0, 0, 512), (1, 0, 256), (1, 256, 512))

TIME_PASSES = TIME // K_PASS
N_HALF = 512
HALVES = TIME // N_HALF

FLOPS = 2 * MODELS * ROWS * FEATURES * SAMPLES + 2 * ROWS * TIME * TIME


def tile_model_pb_k_kernel(tc, h_enc, dec_W, dec_b, map_W, map_b, out):
    nc = tc.nc
    h_rows = h_enc.rearrange("n b c l d -> n (b c l) d")
    out_rows = out.rearrange("b c s -> (b c) s")

    with ExitStack() as ctx:
        keep = ctx.enter_context(tc.tile_pool(name="keep", bufs=1))
        loads = ctx.enter_context(tc.tile_pool(name="loads", bufs=LOAD_BUFS))
        stage = ctx.enter_context(tc.tile_pool(name="stage", bufs=STAGE_BUFS))
        psum_t = ctx.enter_context(tc.psum_pool(name="psum_t", bufs=4))
        psum_r = ctx.enter_context(tc.psum_pool(name="psum_r", bufs=2))
        psum_w = ctx.enter_context(tc.psum_pool(name="psum_w", bufs=2))
        ctx.enter_context(tc.manual_schedule())

        def cut(of_model):
            pieces = []
            for n in range(MODELS):
                first = 0
                for count in of_model[n]:
                    pieces.append((n, first, count))
                    first += count
            return pieces

        steps = cut(STEP_PASSES)
        load_pieces = cut(LOAD_PASSES)

        h_raw = {}
        w_raw = {}
        h_grouped = {}
        w_grouped = {}
        h_mx = {}
        w_mx = {}
        r_acc = {}

        def load(piece):
            if piece in MAP_LOADS:
                load_map(MAP_EARLY[MAP_LOADS.index(piece)])
            n, first, count = load_pieces[piece]
            features = slice(first * K_PASS, (first + count) * K_PASS)
            h_part = loads.tile([ROWS, LOAD_MOST, K_PASS], BF16)
            nc.sync.dma_start(
                out=h_part[:, 0:count].rearrange("r c k -> r (c k)"),
                in_=h_rows[n, :, features],
            )
            w_part = loads.tile([P, LOAD_MOST, PACK, SAMPLES], BF16)
            nc.sync.dma_start(
                out=w_part[:, 0:count].rearrange("q c j w -> q c (j w)"),
                in_=dec_W[n, features, :].rearrange("(c q j) w -> q c (j w)", q=P, j=PACK),
            )
            for c in range(count):
                h_raw[n, first + c] = (h_part, c)
                w_raw[n, first + c] = (w_part, c)

        def transpose_h(i):
            n, first_pass, count = steps[i]
            part, place = h_raw[n, first_pass]
            words = part[:, place : place + count].bitcast(F32).rearrange("r c (q u) -> r c u q", u=2)
            grouped = stage.tile([P, STEP_MOST * ROWS * PACK], BF16, name="h_grouped_sb", align_bytes=64)
            grouped_words = grouped[:].bitcast(F32).rearrange("q (c r u) -> q c r u", c=STEP_MOST, u=2)
            for first in range(0, count, BANK_PASSES):
                bank = psum_t.tile([P, BANK_PASSES, 2, ROWS], F32, name="h_bank")
                for cb in range(BANK_PASSES):
                    for u in range(2):
                        nc.tensor.transpose(bank[:, cb, u, :], words[:, first + cb, u, :], ident_f32[:])
                nc.scalar.copy(
                    out=grouped_words[:, first : first + BANK_PASSES],
                    in_=bank[:].rearrange("q c u r -> q c r u"),
                )
            h_grouped[i] = grouped[:, 0 : count * ROWS * PACK]

        def regroup_w(i):
            n, first_pass, count = steps[i]
            part, place = w_raw[n, first_pass]
            raw = part[:, place : place + count]
            grouped = stage.tile([P, STEP_MOST, SAMPLES, PACK], BF16, name="w_grouped_sb", align_bytes=64)
            nc.vector.tensor_copy(
                out=grouped[:, 0:count, 0:W_COLS_VECTOR, :].rearrange("q c (g i) j -> q c g j i", i=4),
                in_=raw[:, :, :, 0:W_COLS_VECTOR].rearrange("q c j (g i) -> q c g j i", i=4),
            )
            nc.scalar.copy(
                out=grouped[:, 0:count, W_COLS_VECTOR:SAMPLES, :].rearrange("q c (g i) j -> q c g j i", i=4),
                in_=raw[:, :, :, W_COLS_VECTOR:SAMPLES].rearrange("q c j (g i) -> q c g j i", i=4),
            )
            w_grouped[i] = grouped[:, 0:count].rearrange("q c w j -> q (c w j)")

        def quantise(i, values, operand):
            width = steps[i][2] * P
            words = stage.tile([P, STEP_MOST * P], U32, tag=operand + "_words", align_bytes=64)
            scales = stage.tile([P, STEP_MOST * P], U8, tag=operand + "_scales", align_bytes=64)
            nc.vector.quantize_mx(out=words[:, 0:width].bitcast(FP8X4), scales=scales[:, 0:width], in_=values)
            return words, scales

        def multiply(i):
            n, first, count = steps[i]
            if first == 0:
                acc = psum_r.tile([ROWS, SAMPLES], F32, name="r_sums")
                r_acc[n] = acc
            h_words, h_scales = h_mx[i]
            w_words, w_scales = w_mx[i]
            for cp in range(count):
                cols = slice(cp * P, (cp + 1) * P)
                nc.tensor.matmul_mx(
                    out=r_acc[n][:],
                    lhsT=h_words[:, cols].bitcast(FP8X4),
                    lhsT_scale=h_scales[:, cols],
                    rhs=w_words[:, cols].bitcast(FP8X4),
                    rhs_scale=w_scales[:, cols],
                    start=(first + cp == 0),
                    stop=(first + cp == PASSES - 1),
                )

        def finish_model(n):
            nc.vector.tensor_tensor(
                out=x_sb[:].rearrange("r (g j m a) -> r g j m a", g=TIME_PASSES, j=PACK, a=2)[:, :, n % PACK, :, n // PACK],
                in0=r_acc[n][:].rearrange("r (g m) -> r g m", g=TIME_PASSES),
                in1=bias_sb[:, n * SAMPLES : (n + 1) * SAMPLES].rearrange("r (g m) -> r g m", g=TIME_PASSES),
                op=ADD,
            )

        def load_map(part):
            g, half = part
            nc.sync.dma_start(
                out=m_raw[:, g, half],
                in_=map_W[g * K_PASS : (g + 1) * K_PASS, half * N_HALF : (half + 1) * N_HALF].rearrange(
                    "(q j) s -> q j s", j=PACK
                ),
            )

        def regroup_map(part):
            g, half = part
            nc.vector.tensor_copy(
                out=m_grouped[:, g, half, 0:M_COLS_VECTOR, :].rearrange("q (c i) j -> q c j i", i=4),
                in_=m_raw[:, g, half, :, 0:M_COLS_VECTOR].rearrange("q j (c i) -> q c j i", i=4),
            )
            nc.scalar.copy(
                out=m_grouped[:, g, half, M_COLS_VECTOR:N_HALF, :].rearrange("q (c i) j -> q c j i", i=4),
                in_=m_raw[:, g, half, :, M_COLS_VECTOR:N_HALF].rearrange("q j (c i) -> q c j i", i=4),
            )

        def quantise_map(part):
            g, half = part
            nc.vector.quantize_mx(
                out=m_words[:, g, half].bitcast(FP8X4),
                scales=m_scales[:, g, half],
                in_=m_grouped[:, g, half].rearrange("q s j -> q (s j)"),
            )

        def transpose_x(j):
            for g in range(TIME_PASSES):
                first = (g * PACK + j) * P
                nc.tensor.transpose(x_bank[g][:, j, :], x_sb[:, first : first + P], ident_bf16[:])

        def spread_biases():
            for b in range(2):
                bias_bank = psum_w.tile([P, TIME], BF16, tag="wide")
                for half in range(HALVES):
                    cols = slice(half * N_HALF, (half + 1) * N_HALF)
                    nc.tensor.matmul(
                        out=bias_bank[:, cols],
                        lhsT=ones[:],
                        rhs=bias_rows[:, b * TIME + half * N_HALF : b * TIME + (half + 1) * N_HALF],
                        start=True,
                        stop=True,
                    )
                nc.scalar.copy(out=bias_sb[:, b * TIME : (b + 1) * TIME], in_=bias_bank[:])

        m_raw = keep.tile([P, TIME_PASSES, HALVES, PACK, N_HALF], BF16)
        m_grouped = keep.tile([P, TIME_PASSES, HALVES, N_HALF, PACK], BF16, align_bytes=64)
        m_words = keep.tile([P, TIME_PASSES, HALVES, N_HALF], U32, align_bytes=64)
        m_scales = keep.tile([P, TIME_PASSES, HALVES, N_HALF], U8, align_bytes=64)
        bias_rows = keep.tile([P, 2 * TIME], BF16)
        nc.vector.memset(bias_rows[:].bitcast(I32), 0)
        ones = keep.tile([P, P], BF16)
        nc.vector.memset(ones[:], 1.0)
        load(0)
        load(1)
        nc.sync.dma_start(out=bias_rows[0:1, 0:TIME], in_=dec_b.rearrange("n p -> (n p)").unsqueeze(0))
        nc.sync.dma_start(out=bias_rows[0:1, TIME : 2 * TIME], in_=map_b.unsqueeze(0))
        for piece in range(2, LOADS_AHEAD):
            load(piece)

        ident_f32 = keep.tile([P, P], F32)
        make_identity(nc, ident_f32[:])
        ident_bf16 = keep.tile([P, P], BF16)
        make_identity(nc, ident_bf16[:])
        bias_sb = keep.tile([P, 2 * TIME], BF16)

        x_sb = keep.tile([ROWS, TIME], BF16)
        next_load = LOADS_AHEAD
        for i in range(len(steps)):
            if i == BIAS_STEP:
                spread_biases()
            if i in MAP_STEPS:
                regroup_map(MAP_EARLY[MAP_STEPS.index(i)])
            transpose_h(i)
            if i >= MULTIPLY_LAG:
                multiply(i - MULTIPLY_LAG)
            regroup_w(i)
            if i in MAP_STEPS:
                quantise_map(MAP_EARLY[MAP_STEPS.index(i)])
            h_mx[i] = quantise(i, h_grouped[i], "h")
            w_mx[i] = quantise(i, w_grouped[i], "w")
            if i >= MULTIPLY_LAG:
                n, first, count = steps[i - MULTIPLY_LAG]
                if first + count == PASSES:
                    finish_model(n)
            if next_load < len(load_pieces):
                n, first, count = load_pieces[next_load - LOADS_AHEAD]
                if steps[i][0] == n and steps[i][1] + steps[i][2] == first + count:
                    load(next_load)
                    next_load += 1
        for part in MAP_LATE:
            load_map(part)
        x_bank = []
        for g in range(TIME_PASSES):
            bank = psum_w.tile([P, PACK, ROWS], BF16, tag="wide")
            x_bank.append(bank)
        for j in range(PACK - 1):
            transpose_x(j)
        for i in range(len(steps) - MULTIPLY_LAG, len(steps)):
            multiply(i)
        regroup_map(MAP_LATE[0])
        finish_model(MODELS - 1)
        transpose_x(PACK - 1)
        regroup_map(MAP_LATE[1])

        x_grouped = keep.tile([P, TIME_PASSES, ROWS, PACK], BF16, align_bytes=64)
        x_words = keep.tile([P, TIME_PASSES, ROWS], U32, align_bytes=64)
        x_scales = keep.tile([P, TIME_PASSES, ROWS], U8, align_bytes=64)
        for g in range(TIME_PASSES):
            nc.scalar.copy(out=x_grouped[:, g], in_=x_bank[g][:].rearrange("q j r -> q r j"))
        quantise_map(MAP_LATE[0])
        for g in range(TIME_PASSES):
            nc.vector.quantize_mx(
                out=x_words[:, g].bitcast(FP8X4),
                scales=x_scales[:, g],
                in_=x_grouped[:, g].rearrange("q r j -> q (r j)"),
            )
        quantise_map(MAP_LATE[1])
        y_acc = []
        for half in range(HALVES):
            y_bank = psum_w.tile([ROWS, N_HALF], F32, tag="wide")
            y_acc.append(y_bank)
        for half in range(HALVES):
            for g in range(TIME_PASSES):
                nc.tensor.matmul_mx(
                    out=y_acc[half][:],
                    lhsT=x_words[:, g].bitcast(FP8X4),
                    lhsT_scale=x_scales[:, g],
                    rhs=m_words[:, g, half].bitcast(FP8X4),
                    rhs_scale=m_scales[:, g, half],
                    start=(g == 0),
                    stop=(g == TIME_PASSES - 1),
                )
        for half, first, end in OUT_PIECES:
            y_sb = stage.tile([ROWS, N_HALF], F32)
            nc.vector.tensor_tensor(
                out=y_sb[:, 0 : end - first],
                in0=y_acc[half][:, first:end],
                in1=bias_sb[:, TIME + half * N_HALF + first : TIME + half * N_HALF + end],
                op=ADD,
            )
            nc.sync.dma_start(out=out_rows[:, half * N_HALF + first : half * N_HALF + end], in_=y_sb[:, 0 : end - first])
